import numpy as np
import ml_dtypes


def mxq(x, axis, fmt="e4m3"):
    dtype, down = {"e4m3": (ml_dtypes.float8_e4m3fn, 7), "e5m2": (ml_dtypes.float8_e5m2, 14)}[fmt]
    v = np.moveaxis(np.asarray(x, np.float32).astype(ml_dtypes.bfloat16).astype(np.float64), axis, -1)
    blocks = v.reshape(v.shape[:-1] + (-1, 32))
    amax = np.abs(blocks).max(-1, keepdims=True)
    byte = np.maximum(np.where(amax > 0, np.frexp(amax)[1] - 1 + 127, 0) - down, 1)
    scale = np.exp2(byte - 127.0)
    codes = (blocks / scale).astype(np.float32).astype(dtype).astype(np.float64)
    return np.moveaxis((codes * scale).reshape(v.shape), -1, axis)


WIDE = False


def mx_kscale(k):
    if not WIDE:
        return np.ones(k)
    levels = np.array([10, -10, 5, -5, 0])
    if k % 512:
        return np.exp2(np.random.permutation(np.resize(levels, k // 32))).repeat(32)
    a = np.empty((k // 512, 16))
    for p in range(k // 512):
        a[p, :8] = np.random.permutation(np.resize(levels, 8))
        for g in range(8):
            far = levels[np.abs(levels - a[p, g]) >= 10]
            a[p, g + 8] = far[np.random.randint(len(far))]
    return np.exp2(a.ravel()).repeat(32)


BF16 = ml_dtypes.bfloat16


def bf(x):
    return np.asarray(x, np.float32).astype(BF16)


def f64(x):
    return np.asarray(x).astype(np.float64)


B, T, HS, C, NH, HD, WS, MAXD = 1, 8, 28, 512, 32, 16, 7, 3
N = T * HS * HS
E = NH * HD
BT = B * NH * T
EPS = 1e-12


def l2norm(v, axis):
    return v / np.maximum(np.sqrt(np.sum(v * v, axis=axis, keepdims=True)), EPS)


def setup_inputs():
    s = mx_kscale(C)
    return {"x": bf(np.random.standard_normal((B, N, C)) * s),
            "q_w": bf(np.random.standard_normal((E, C)) / np.sqrt(C) / s),
            "k_w": bf(np.random.standard_normal((E, C)) / np.sqrt(C) / s)}


def reference(x, q_w, k_w):
    xq = mxq(f64(x), 2, "e4m3")
    q = xq @ mxq(f64(q_w), 1, "e4m3").T
    k = xq @ mxq(f64(k_w), 1, "e4m3").T
    q = q.reshape(B, N, NH, HD).transpose(0, 2, 1, 3)
    k = k.reshape(B, N, NH, HD).transpose(0, 2, 1, 3)
    q = q.reshape(B * NH, T, HS, HS, HD).transpose(0, 1, 4, 2, 3)
    k = k.reshape(B * NH, T, HS, HS, HD).transpose(0, 1, 4, 2, 3)
    k_post = np.concatenate([k[:, 1:], k[:, -1:]], axis=1)
    qp = l2norm(q.reshape(BT, HD, HS, HS), 1)
    kp = l2norm(k_post.reshape(BT, HD, HS, HS), 1)
    return qp, kp

@@ -1,0 +1,264 @@
+from contextlib import ExitStack
+
+import concourse.mybir as mybir
+from concourse.masks import make_identity
+
+F32 = mybir.dt.float32
+BF16 = mybir.dt.bfloat16
+U32 = mybir.dt.uint32
+U8 = mybir.dt.uint8
+FP8X4 = mybir.dt.float8_e4m3fn_x4
+ALU = mybir.AluOpType
+ACT = mybir.ActivationFunctionType
+
+P = 128
+PACK = 4
+HALVES = 2
+C = 512
+T = 8
+FRAME = 784
+TOKENS = T * FRAME
+HEADS = 32
+D_LO = 4
+D_HI = 4
+GROUP = 256
+GROUPS = (TOKENS + GROUP - 1) // GROUP
+BANK_HI = 2
+BLOCK = 4
+BLOCK_TOKENS = BLOCK * P
+BLOCKS = (TOKENS + BLOCK_TOKENS - 1) // BLOCK_TOKENS
+BANK_ROWS = 2
+MAX_INV_NORM = 1.0e12
+LAG_SUM = 3
+LAG_NORM = 5
+LAG_SCALE = 6
+AHEAD = 4
+KEY_LEAD = 2
+
+FLOPS = 2 * TOKENS * C * (2 * HEADS * D_LO * D_HI)
+
+
+def turn_rows(nc, banks, stage, identity, rows):
+    sets = rows.shape[1]
+    grouped = stage.tile([P, BLOCK * P * PACK], BF16, align_bytes=64)
+    grouped_words = grouped[:].bitcast(F32).rearrange("p (g r u) -> p g r u", r=P, u=HALVES)
+    for first in range(0, sets, BANK_ROWS):
+        count = min(BANK_ROWS, sets - first)
+        turned = banks.tile([P, BANK_ROWS, HALVES, P], F32, tag="bank")
+        for g in range(count):
+            row_words = rows[:, first + g, :].bitcast(F32)
+            for u in range(HALVES):
+                nc.tensor.transpose(turned[:, g, u, :], row_words[:, u::HALVES], identity[:])
+        copy_out = nc.vector.tensor_copy if (first // BANK_ROWS) % 2 == 0 else nc.scalar.copy
+        copy_out(
+            grouped_words[:, first : first + count],
+            turned[:, 0:count].rearrange("p g u r -> p g r u"),
+        )
+    return grouped[:, 0 : sets * P * PACK]
+
+
+def quantise(nc, grouped, codes, scales):
+    nc.vector.quantize_mx(out=codes.bitcast(FP8X4), scales=scales, in_=grouped)
+
+
+def frame_pieces(group):
+    start = group * GROUP
+    end = min(start + GROUP, TOKENS)
+    return [
+        (frame, max(start, frame * FRAME), min(end, (frame + 1) * FRAME))
+        for frame in range(start // FRAME, (end - 1) // FRAME + 1)
+    ]
+
+
+def frames_fed(shift, frame):
+    return [t for t in range(T) if min(t + shift, T - 1) == frame]
+
+
+def tile_costvolumeattention17_pa_kernel(tc, x, q_w, k_w, out_0, out_1):
+    nc = tc.nc
+    with ExitStack() as ctx:
+        keep = ctx.enter_context(tc.tile_pool(name="keep", bufs=1))
+        loads = ctx.enter_context(tc.tile_pool(name="loads", bufs=BLOCKS))
+        stage = ctx.enter_context(tc.tile_pool(name="stage", bufs=3))
+        norm = ctx.enter_context(tc.tile_pool(name="norm", bufs=4))
+        frames = ctx.enter_context(tc.tile_pool(name="frames", bufs=3))
+        banks = ctx.enter_context(tc.psum_pool(name="banks", bufs=8))
+        ctx.enter_context(tc.manual_schedule())
+
+        w_codes = {}
+        w_scales = {}
+        for name in ("q", "k"):
+            w_codes[name] = keep.tile([P, D_HI * P], U32, align_bytes=64, name="w_codes_" + name)
+            w_scales[name] = keep.tile([P, D_HI * P], U8, align_bytes=64, name="w_scales_" + name)
+        x_codes = keep.tile([P, TOKENS], U32, align_bytes=64)
+        x_scales = keep.tile([P, TOKENS], U8, align_bytes=64)
+
+        outputs = {
+            "q": out_0.rearrange("(h t) (dlo dhi) i j -> t h dlo (dhi i j)", t=T, dlo=D_LO),
+            "k": out_1.rearrange("(h t) (dlo dhi) i j -> t h dlo (dhi i j)", t=T, dlo=D_LO),
+        }
+        shifts = {"q": 0, "k": 1}
+
+        items = []
+        for last_frame in range(-KEY_LEAD, T):
+            for name, lead in (("q", 0), ("k", KEY_LEAD)):
+                for group in range(GROUPS):
+                    pieces = [piece for piece in frame_pieces(group) if frames_fed(shifts[name], piece[0])]
+                    if pieces and frame_pieces(group)[-1][0] == last_frame + lead:
+                        items.append((group, name, pieces))
+
+        x_rows = x[0].rearrange("(a p) c -> p a c", p=P)
+        weights = {"q": q_w, "k": k_w}
+        jobs = []
+        seen = []
+        for i, (group, name, pieces) in enumerate(items):
+            if name not in seen:
+                seen.append(name)
+                w_rows = keep.tile([P, D_HI, C], BF16, name="w_rows_" + name)
+                nc.sync.dma_start(out=w_rows[:], in_=weights[name].rearrange("(m j) c -> m j c", j=D_HI))
+                jobs.append((w_rows, w_codes[name][:], w_scales[name][:], i))
+            block = group * GROUP // BLOCK_TOKENS
+            if block not in seen:
+                seen.append(block)
+                first = block * BLOCK
+                count = min(BLOCK, TOKENS // P - first)
+                x_block = loads.tile([P, count, C], BF16, tag="x_block")
+                nc.sync.dma_start(out=x_block[:], in_=x_rows[:, first : first + count, :])
+                columns = slice(first * P, (first + count) * P)
+                jobs.append((x_block, x_codes[:, columns], x_scales[:, columns], i))
+
+        identity = keep.tile([P, P], F32)
+        make_identity(nc, identity[:])
+        same_head = keep.tile([P, HEADS], F32)
+        nc.vector.tensor_reduce(
+            out=same_head[:],
+            in_=identity[:].rearrange("p (h i) -> p h i", i=D_LO),
+            axis=mybir.AxisListType.X,
+            op=ALU.add,
+        )
+        ones_lo = keep.tile([P, HEADS, D_LO], F32)
+        nc.vector.tensor_copy(out=ones_lo[:], in_=same_head[:].unsqueeze(2).to_broadcast([P, HEADS, D_LO]))
+
+        pair_sums = {}
+        hi_sums = {}
+        inv_norms = {}
+        frame_tiles = {}
+
+        def width_of(i):
+            return min(GROUP, TOKENS - items[i][0] * GROUP)
+
+        def multiply(i, first_hi):
+            group, name, pieces = items[i]
+            tokens = slice(group * GROUP, group * GROUP + width_of(i))
+            product = banks.tile([P, BANK_HI, GROUP], F32, tag="bank")
+            for j in range(BANK_HI):
+                channels = slice((first_hi + j) * P, (first_hi + j + 1) * P)
+                nc.tensor.matmul_mx(
+                    out=product[:, j, 0 : width_of(i)],
+                    lhsT=w_codes[name][:, channels].bitcast(FP8X4),
+                    lhsT_scale=w_scales[name][:, channels],
+                    rhs=x_codes[:, tokens].bitcast(FP8X4),
+                    rhs_scale=x_scales[:, tokens],
+                    start=True,
+                    stop=True,
+                )
+            return product
+
+        def square(i):
+            width = width_of(i)
+            squares = norm.tile([P, D_HI, GROUP], F32, bufs=3)
+            for first_hi in range(0, D_HI, BANK_HI):
+                product = multiply(i, first_hi)
+                nc.scalar.activation(
+                    out=squares[:, first_hi : first_hi + BANK_HI, 0:width],
+                    in_=product[:, :, 0:width],
+                    func=ACT.Square,
+                )
+            pair_sums[i] = norm.tile([P, D_HI // 2, GROUP], F32, name="pair_sums", bufs=LAG_SUM + 2)
+            nc.gpsimd.tensor_tensor(
+                out=pair_sums[i][:, :, 0:width],
+                in0=squares[:, 0:2, 0:width],
+                in1=squares[:, 2:4, 0:width],
+                op=ALU.add,
+            )
+
+        def finish_sum(i):
+            width = width_of(i)
+            hi_sums[i] = norm.tile([P, GROUP], F32, name="hi_sums", bufs=LAG_NORM - LAG_SUM + 2)
+            nc.vector.tensor_tensor(
+                out=hi_sums[i][:, 0:width],
+                in0=pair_sums[i][:, 0, 0:width],
+                in1=pair_sums[i][:, 1, 0:width],
+                op=ALU.add,
+            )
+
+        def invert_norm(i):
+            width = width_of(i)
+            head_sums = banks.tile([P, GROUP], F32, tag="bank")
+            nc.tensor.matmul(
+                out=head_sums[:, 0:width],
+                lhsT=ones_lo[:].rearrange("p h i -> p (h i)"),
+                rhs=hi_sums[i][:, 0:width],
+                start=True,
+                stop=True,
+            )
+            inv_norms[i] = norm.tile([P, GROUP], F32, name="inv_norm", bufs=LAG_SCALE - LAG_NORM + 2)
+            nc.scalar.activation(
+                out=inv_norms[i][:, 0:width], in_=head_sums[:, 0:width], func=ACT.Abs_reciprocal_sqrt
+            )
+
+        def store(name, frame, frame_tile, first, end):
+            for t in frames_fed(shifts[name], frame):
+                nc.sync.dma_start(
+                    out=outputs[name][t],
+                    in_=frame_tile[:].rearrange("p j n -> p (j n)"),
+                )
+
+        def scale_and_store(i):
+            group, name, pieces = items[i]
+            if pieces[0][1] == pieces[0][0] * FRAME:
+                frame_tiles[name] = [frames.tile([P, D_HI, FRAME], F32, name="frame_" + name)]
+            if len(pieces) > 1:
+                frame_tiles[name].append(frames.tile([P, D_HI, FRAME], F32, name="frame_" + name))
+            for first_hi in range(0, D_HI, BANK_HI):
+                product = multiply(i, first_hi)
+                for frame_tile, (frame, start, end) in zip(frame_tiles[name], pieces):
+                    columns = slice(start - group * GROUP, end - group * GROUP)
+                    nc.vector.scalar_tensor_tensor(
+                        out=frame_tile[:, first_hi : first_hi + BANK_HI, start - frame * FRAME : end - frame * FRAME],
+                        in0=inv_norms[i][:, columns].unsqueeze(1).to_broadcast([P, BANK_HI, end - start]),
+                        scalar=MAX_INV_NORM,
+                        in1=product[:, :, columns],
+                        op0=ALU.min,
+                        op1=ALU.mult,
+                    )
+            for frame_tile, (frame, start, end) in zip(list(frame_tiles[name]), pieces):
+                if end == (frame + 1) * FRAME:
+                    store(name, frame, frame_tile, 0, FRAME)
+                if end == (frame + 1) * FRAME:
+                    frame_tiles[name] = frame_tiles[name][1:]
+
+        at_once = [job for job in jobs if job[3] == 0]
+        turned_rows = [turn_rows(nc, banks, stage, identity, job[0]) for job in at_once]
+        for job, grouped in zip(at_once, turned_rows):
+            quantise(nc, grouped, job[1], job[2])
+        later = [job for job in jobs if job[3] > 0]
+
+        waiting = []
+        next_job = 0
+        for step in range(len(items) + LAG_SCALE):
+            if step < len(items):
+                for job, grouped in waiting:
+                    quantise(nc, grouped, job[1], job[2])
+                waiting = []
+                if next_job < len(later) and later[next_job][3] <= step + AHEAD:
+                    job = later[next_job]
+                    next_job += 1
+                    waiting = [(job, turn_rows(nc, banks, stage, identity, job[0]))]
+                square(step)
+            if 0 <= step - LAG_SUM < len(items):
+                finish_sum(step - LAG_SUM)
+            if 0 <= step - LAG_NORM < len(items):
+                invert_norm(step - LAG_NORM)
+            if 0 <= step - LAG_SCALE < len(items):
+                scale_and_store(step - LAG_SCALE)

@@ -29,36 +29,15 @@ BLOCK_TOKENS = BLOCK * P
 BLOCKS = (TOKENS + BLOCK_TOKENS - 1) // BLOCK_TOKENS
 BANK_ROWS = 2
 MAX_INV_NORM = 1.0e12
-LAG_SUM = 3
-LAG_NORM = 5
-LAG_SCALE = 6
-AHEAD = 4
-KEY_LEAD = 2
+LAG_SUM = 1
+LAG_NORM = 2
+LAG_SCALE = 3
+HEAD_STEPS = LAG_SCALE + 1
+HEAD_PARTS = 3
+LATER_PARTS = 2
+KEY_LEAD = 3
 
 FLOPS = 2 * TOKENS * C * (2 * HEADS * D_LO * D_HI)
-
-
-def turn_rows(nc, banks, stage, identity, rows):
-    sets = rows.shape[1]
-    grouped = stage.tile([P, BLOCK * P * PACK], BF16, align_bytes=64)
-    grouped_words = grouped[:].bitcast(F32).rearrange("p (g r u) -> p g r u", r=P, u=HALVES)
-    for first in range(0, sets, BANK_ROWS):
-        count = min(BANK_ROWS, sets - first)
-        turned = banks.tile([P, BANK_ROWS, HALVES, P], F32, tag="bank")
-        for g in range(count):
-            row_words = rows[:, first + g, :].bitcast(F32)
-            for u in range(HALVES):
-                nc.tensor.transpose(turned[:, g, u, :], row_words[:, u::HALVES], identity[:])
-        copy_out = nc.vector.tensor_copy if (first // BANK_ROWS) % 2 == 0 else nc.scalar.copy
-        copy_out(
-            grouped_words[:, first : first + count],
-            turned[:, 0:count].rearrange("p g u r -> p g r u"),
-        )
-    return grouped[:, 0 : sets * P * PACK]
-
-
-def quantise(nc, grouped, codes, scales):
-    nc.vector.quantize_mx(out=codes.bitcast(FP8X4), scales=scales, in_=grouped)
 
 
 def frame_pieces(group):
@@ -98,6 +77,7 @@ def tile_costvolumeattention17_pa_kernel(tc, x, q_w, k_w, out_0, out_1):
             "k": out_1.rearrange("(h t) (dlo dhi) i j -> t h dlo (dhi i j)", t=T, dlo=D_LO),
         }
         shifts = {"q": 0, "k": 1}
+        last_frame_q = out_0.rearrange("(h t) d i j -> t h d (i j)", t=T)[T - 1]
 
         items = []
         for last_frame in range(-KEY_LEAD, T):
@@ -139,6 +119,7 @@ def tile_costvolumeattention17_pa_kernel(tc, x, q_w, k_w, out_0, out_1):
         ones_lo = keep.tile([P, HEADS, D_LO], F32)
         nc.vector.tensor_copy(out=ones_lo[:], in_=same_head[:].unsqueeze(2).to_broadcast([P, HEADS, D_LO]))
 
+        squares = {}
         pair_sums = {}
         hi_sums = {}
         inv_norms = {}
@@ -164,23 +145,24 @@ def tile_costvolumeattention17_pa_kernel(tc, x, q_w, k_w, out_0, out_1):
                 )
             return product
 
-        def square(i):
+        def square(i, first_hi):
             width = width_of(i)
-            squares = norm.tile([P, D_HI, GROUP], F32, bufs=3)
-            for first_hi in range(0, D_HI, BANK_HI):
-                product = multiply(i, first_hi)
-                nc.scalar.activation(
-                    out=squares[:, first_hi : first_hi + BANK_HI, 0:width],
-                    in_=product[:, :, 0:width],
-                    func=ACT.Square,
-                )
-            pair_sums[i] = norm.tile([P, D_HI // 2, GROUP], F32, name="pair_sums", bufs=LAG_SUM + 2)
-            nc.gpsimd.tensor_tensor(
-                out=pair_sums[i][:, :, 0:width],
-                in0=squares[:, 0:2, 0:width],
-                in1=squares[:, 2:4, 0:width],
-                op=ALU.add,
+            if first_hi == 0:
+                squares[i] = norm.tile([P, D_HI, GROUP], F32, name="squares", bufs=3)
+            product = multiply(i, first_hi)
+            nc.scalar.activation(
+                out=squares[i][:, first_hi : first_hi + BANK_HI, 0:width],
+                in_=product[:, :, 0:width],
+                func=ACT.Square,
             )
+            if first_hi + BANK_HI == D_HI:
+                pair_sums[i] = norm.tile([P, D_HI // 2, GROUP], F32, name="pair_sums", bufs=LAG_SUM + 2)
+                nc.gpsimd.tensor_tensor(
+                    out=pair_sums[i][:, :, 0:width],
+                    in0=squares[i][:, 0:2, 0:width],
+                    in1=squares[i][:, 2:4, 0:width],
+                    op=ALU.add,
+                )
 
         def finish_sum(i):
             width = width_of(i)
@@ -207,58 +189,89 @@ def tile_costvolumeattention17_pa_kernel(tc, x, q_w, k_w, out_0, out_1):
                 out=inv_norms[i][:, 0:width], in_=head_sums[:, 0:width], func=ACT.Abs_reciprocal_sqrt
             )
 
-        def store(name, frame, frame_tile, first, end):
-            for t in frames_fed(shifts[name], frame):
-                nc.sync.dma_start(
-                    out=outputs[name][t],
-                    in_=frame_tile[:].rearrange("p j n -> p (j n)"),
-                )
-
-        def scale_and_store(i):
+        def open_frames(i):
             group, name, pieces = items[i]
             if pieces[0][1] == pieces[0][0] * FRAME:
                 frame_tiles[name] = [frames.tile([P, D_HI, FRAME], F32, name="frame_" + name)]
             if len(pieces) > 1:
                 frame_tiles[name].append(frames.tile([P, D_HI, FRAME], F32, name="frame_" + name))
-            for first_hi in range(0, D_HI, BANK_HI):
-                product = multiply(i, first_hi)
-                for frame_tile, (frame, start, end) in zip(frame_tiles[name], pieces):
-                    columns = slice(start - group * GROUP, end - group * GROUP)
-                    nc.vector.scalar_tensor_tensor(
-                        out=frame_tile[:, first_hi : first_hi + BANK_HI, start - frame * FRAME : end - frame * FRAME],
-                        in0=inv_norms[i][:, columns].unsqueeze(1).to_broadcast([P, BANK_HI, end - start]),
-                        scalar=MAX_INV_NORM,
-                        in1=product[:, :, columns],
-                        op0=ALU.min,
-                        op1=ALU.mult,
-                    )
+
+        def scale(i, first_hi):
+            group, name, pieces = items[i]
+            product = multiply(i, first_hi)
+            for frame_tile, (frame, start, end) in zip(frame_tiles[name], pieces):
+                columns = slice(start - group * GROUP, end - group * GROUP)
+                nc.vector.scalar_tensor_tensor(
+                    out=frame_tile[:, first_hi : first_hi + BANK_HI, start - frame * FRAME : end - frame * FRAME],
+                    in0=inv_norms[i][:, columns].unsqueeze(1).to_broadcast([P, BANK_HI, end - start]),
+                    scalar=MAX_INV_NORM,
+                    in1=product[:, :, columns],
+                    op0=ALU.min,
+                    op1=ALU.mult,
+                )
+
+        def store(i):
+            group, name, pieces = items[i]
             for frame_tile, (frame, start, end) in zip(list(frame_tiles[name]), pieces):
-                if end == (frame + 1) * FRAME:
-                    store(name, frame, frame_tile, 0, FRAME)
+                whole = not (name == "q" and frame == T - 1)
+                for t in frames_fed(shifts[name], frame):
+                    if whole and end == (frame + 1) * FRAME:
+                        nc.sync.dma_start(out=outputs[name][t], in_=frame_tile[:].rearrange("p j n -> p (j n)"))
+                    if not whole:
+                        first, last = start - frame * FRAME, end - frame * FRAME
+                        nc.sync.dma_start(out=last_frame_q[:, :, first:last], in_=frame_tile[:, :, first:last])
                 if end == (frame + 1) * FRAME:
                     frame_tiles[name] = frame_tiles[name][1:]
 
-        at_once = [job for job in jobs if job[3] == 0]
-        turned_rows = [turn_rows(nc, banks, stage, identity, job[0]) for job in at_once]
-        for job, grouped in zip(at_once, turned_rows):
-            quantise(nc, grouped, job[1], job[2])
-        later = [job for job in jobs if job[3] > 0]
+        parts = []
+        for job in jobs:
+            grouped = []
+            for first in range(0, job[0].shape[1], BANK_ROWS):
+                parts.append((job, grouped, first))
+            parts.append((job, grouped, None))
 
-        waiting = []
-        next_job = 0
+        def prepare(part, copy_out):
+            (rows, codes, scales, first_item), grouped, first = part
+            sets = rows.shape[1]
+            if not grouped:
+                grouped.append(stage.tile([P, BLOCK * P * PACK], BF16, align_bytes=64, name="grouped"))
+            if first is None:
+                nc.vector.quantize_mx(out=codes.bitcast(FP8X4), scales=scales, in_=grouped[0][:, 0 : sets * P * PACK])
+                return
+            grouped_words = grouped[0][:].bitcast(F32).rearrange("p (g r u) -> p g r u", r=P, u=HALVES)
+            count = min(BANK_ROWS, sets - first)
+            turned = banks.tile([P, BANK_ROWS, HALVES, P], F32, tag="bank")
+            for g in range(count):
+                row_words = rows[:, first + g, :].bitcast(F32)
+                for u in range(HALVES):
+                    nc.tensor.transpose(turned[:, g, u, :], row_words[:, u::HALVES], identity[:])
+            copy_out(
+                grouped_words[:, first : first + count],
+                turned[:, 0:count].rearrange("p g u r -> p g r u"),
+            )
+
+        copies = (nc.vector.tensor_copy, nc.scalar.copy)
+        next_part = 0
+        while parts[next_part][0][3] == 0:
+            prepare(parts[next_part], copies[next_part % 2])
+            next_part += 1
+
         for step in range(len(items) + LAG_SCALE):
+            for j in range(HEAD_PARTS if step < HEAD_STEPS else LATER_PARTS):
+                if next_part < len(parts):
+                    by_vector = step < HEAD_STEPS or next_part % 4 == 0
+                    prepare(parts[next_part], nc.vector.tensor_copy if by_vector else nc.scalar.copy)
+                    next_part += 1
             if step < len(items):
-                for job, grouped in waiting:
-                    quantise(nc, grouped, job[1], job[2])
-                waiting = []
-                if next_job < len(later) and later[next_job][3] <= step + AHEAD:
-                    job = later[next_job]
-                    next_job += 1
-                    waiting = [(job, turn_rows(nc, banks, stage, identity, job[0]))]
-                square(step)
+                square(step, 0)
+            if step >= LAG_SCALE:
+                open_frames(step - LAG_SCALE)
+                scale(step - LAG_SCALE, 0)
+                scale(step - LAG_SCALE, BANK_HI)
+                store(step - LAG_SCALE)
             if 0 <= step - LAG_SUM < len(items):
                 finish_sum(step - LAG_SUM)
+            if step < len(items):
+                square(step, BANK_HI)
             if 0 <= step - LAG_NORM < len(items):
                 invert_norm(step - LAG_NORM)
-            if 0 <= step - LAG_SCALE < len(items):
-                scale_and_store(step - LAG_SCALE)

@@ -29,13 +29,13 @@ BLOCK_TOKENS = BLOCK * P
 BLOCKS = (TOKENS + BLOCK_TOKENS - 1) // BLOCK_TOKENS
 BANK_ROWS = 2
 MAX_INV_NORM = 1.0e12
-LAG_SUM = 1
-LAG_NORM = 2
-LAG_SCALE = 3
+LAG_SUM = 3
+LAG_NORM = 5
+LAG_SCALE = 5
 HEAD_STEPS = LAG_SCALE + 1
 HEAD_PARTS = 3
-LATER_PARTS = 2
-KEY_LEAD = 3
+LATER_PARTS = 1
+KEY_LEAD = 4
 
 FLOPS = 2 * TOKENS * C * (2 * HEADS * D_LO * D_HI)
 
@@ -122,6 +122,7 @@ def tile_costvolumeattention17_pa_kernel(tc, x, q_w, k_w, out_0, out_1):
         squares = {}
         pair_sums = {}
         hi_sums = {}
+        head_sums = {}
         inv_norms = {}
         frame_tiles = {}
 
@@ -174,19 +175,22 @@ def tile_costvolumeattention17_pa_kernel(tc, x, q_w, k_w, out_0, out_1):
                 op=ALU.add,
             )
 
-        def invert_norm(i):
+        def sum_heads(i):
             width = width_of(i)
-            head_sums = banks.tile([P, GROUP], F32, tag="bank")
+            head_sums[i] = banks.tile([P, GROUP], F32, name="head_sums", tag="bank")
             nc.tensor.matmul(
-                out=head_sums[:, 0:width],
+                out=head_sums[i][:, 0:width],
                 lhsT=ones_lo[:].rearrange("p h i -> p (h i)"),
                 rhs=hi_sums[i][:, 0:width],
                 start=True,
                 stop=True,
             )
+
+        def invert_norm(i):
+            width = width_of(i)
             inv_norms[i] = norm.tile([P, GROUP], F32, name="inv_norm", bufs=LAG_SCALE - LAG_NORM + 2)
             nc.scalar.activation(
-                out=inv_norms[i][:, 0:width], in_=head_sums[:, 0:width], func=ACT.Abs_reciprocal_sqrt
+                out=inv_norms[i][:, 0:width], in_=head_sums[i][:, 0:width], func=ACT.Abs_reciprocal_sqrt
             )
 
         def open_frames(i):
@@ -257,21 +261,24 @@ def tile_costvolumeattention17_pa_kernel(tc, x, q_w, k_w, out_0, out_1):
             next_part += 1
 
         for step in range(len(items) + LAG_SCALE):
+            new, old = step, step - LAG_SCALE
+            if 0 <= step - LAG_NORM < len(items):
+                sum_heads(step - LAG_NORM)
+            if 0 <= step - LAG_SUM < len(items):
+                finish_sum(step - LAG_SUM)
+            if 0 <= step - LAG_NORM < len(items):
+                invert_norm(step - LAG_NORM)
             for j in range(HEAD_PARTS if step < HEAD_STEPS else LATER_PARTS):
                 if next_part < len(parts):
                     by_vector = step < HEAD_STEPS or next_part % 4 == 0
                     prepare(parts[next_part], nc.vector.tensor_copy if by_vector else nc.scalar.copy)
                     next_part += 1
-            if step < len(items):
-                square(step, 0)
-            if step >= LAG_SCALE:
-                open_frames(step - LAG_SCALE)
-                scale(step - LAG_SCALE, 0)
-                scale(step - LAG_SCALE, BANK_HI)
-                store(step - LAG_SCALE)
-            if 0 <= step - LAG_SUM < len(items):
-                finish_sum(step - LAG_SUM)
-            if step < len(items):
-                square(step, BANK_HI)
-            if 0 <= step - LAG_NORM < len(items):
-                invert_norm(step - LAG_NORM)
+            if old >= 0:
+                open_frames(old)
+            for first_hi in range(0, D_HI, BANK_HI):
+                if new < len(items):
+                    square(new, first_hi)
+                if old >= 0:
+                    scale(old, first_hi)
+            if old >= 0:
+                store(old)

@@ -35,17 +35,22 @@ LAG_SCALE = 5
 HEAD_STEPS = LAG_SCALE + 1
 HEAD_PARTS = 3
 LATER_PARTS = 1
-KEY_LEAD = 4
+ALIGN = 64
+KEY_LEAD = 3
+PIECEWISE = [("k", T - 1), ("q", T - 2), ("q", T - 1)]
 
 FLOPS = 2 * TOKENS * C * (2 * HEADS * D_LO * D_HI)
 
 
-def frame_pieces(group):
-    start = group * GROUP
-    end = min(start + GROUP, TOKENS)
+def windows(start, end):
+    return [(first, min(GROUP, end - first)) for first in range(start, end, GROUP)]
+
+
+def frame_pieces(start, width, frames):
     return [
-        (frame, max(start, frame * FRAME), min(end, (frame + 1) * FRAME))
-        for frame in range(start // FRAME, (end - 1) // FRAME + 1)
+        (frame, max(start, frame * FRAME), min(start + width, (frame + 1) * FRAME))
+        for frame in frames
+        if start < (frame + 1) * FRAME and frame * FRAME < start + width
     ]
 
 
@@ -77,28 +82,45 @@ def tile_costvolumeattention17_pa_kernel(tc, x, q_w, k_w, out_0, out_1):
             "k": out_1.rearrange("(h t) (dlo dhi) i j -> t h dlo (dhi i j)", t=T, dlo=D_LO),
         }
         shifts = {"q": 0, "k": 1}
-        last_frame_q = out_0.rearrange("(h t) d i j -> t h d (i j)", t=T)[T - 1]
+        by_channel = {
+            "q": out_0.rearrange("(h t) d i j -> t h d (i j)", t=T),
+            "k": out_1.rearrange("(h t) d i j -> t h d (i j)", t=T),
+        }
 
+        last = T - 1
+        runs = [
+            ("k", windows(last * FRAME // ALIGN * ALIGN, TOKENS), [last]),
+            ("q", windows(0, TOKENS), range(T)),
+            ("k", windows(FRAME // ALIGN * ALIGN, -(-last * FRAME // ALIGN) * ALIGN), range(1, last)),
+        ]
+        order = [("k", last)]
+        for frame in range(T):
+            order.append(("q", frame))
+            if frame + KEY_LEAD < last:
+                order.append(("k", frame + KEY_LEAD))
+            if frame == 0:
+                order[1:1] = [("k", f) for f in range(1, KEY_LEAD)]
         items = []
-        for last_frame in range(-KEY_LEAD, T):
-            for name, lead in (("q", 0), ("k", KEY_LEAD)):
-                for group in range(GROUPS):
-                    pieces = [piece for piece in frame_pieces(group) if frames_fed(shifts[name], piece[0])]
-                    if pieces and frame_pieces(group)[-1][0] == last_frame + lead:
-                        items.append((group, name, pieces))
+        for name, frame in order:
+            for run_name, run, run_frames in runs:
+                for start, width in run:
+                    pieces = frame_pieces(start, width, run_frames)
+                    if run_name == name and pieces[-1][0] == frame:
+                        items.append((start, width, name, pieces))
 
         x_rows = x[0].rearrange("(a p) c -> p a c", p=P)
         weights = {"q": q_w, "k": k_w}
         jobs = []
         seen = []
-        for i, (group, name, pieces) in enumerate(items):
+        for i, (start, width, name, pieces) in enumerate(items):
             if name not in seen:
                 seen.append(name)
                 w_rows = keep.tile([P, D_HI, C], BF16, name="w_rows_" + name)
                 nc.sync.dma_start(out=w_rows[:], in_=weights[name].rearrange("(m j) c -> m j c", j=D_HI))
                 jobs.append((w_rows, w_codes[name][:], w_scales[name][:], i))
-            block = group * GROUP // BLOCK_TOKENS
-            if block not in seen:
+            for block in range(start // BLOCK_TOKENS, (start + width - 1) // BLOCK_TOKENS + 1):
+                if block in seen:
+                    continue
                 seen.append(block)
                 first = block * BLOCK
                 count = min(BLOCK, TOKENS // P - first)
@@ -127,11 +149,11 @@ def tile_costvolumeattention17_pa_kernel(tc, x, q_w, k_w, out_0, out_1):
         frame_tiles = {}
 
         def width_of(i):
-            return min(GROUP, TOKENS - items[i][0] * GROUP)
+            return items[i][1]
 
         def multiply(i, first_hi):
-            group, name, pieces = items[i]
-            tokens = slice(group * GROUP, group * GROUP + width_of(i))
+            base, width, name, pieces = items[i]
+            tokens = slice(base, base + width)
             product = banks.tile([P, BANK_HI, GROUP], F32, tag="bank")
             for j in range(BANK_HI):
                 channels = slice((first_hi + j) * P, (first_hi + j + 1) * P)
@@ -194,17 +216,17 @@ def tile_costvolumeattention17_pa_kernel(tc, x, q_w, k_w, out_0, out_1):
             )
 
         def open_frames(i):
-            group, name, pieces = items[i]
+            base, width, name, pieces = items[i]
             if pieces[0][1] == pieces[0][0] * FRAME:
                 frame_tiles[name] = [frames.tile([P, D_HI, FRAME], F32, name="frame_" + name)]
             if len(pieces) > 1:
                 frame_tiles[name].append(frames.tile([P, D_HI, FRAME], F32, name="frame_" + name))
 
         def scale(i, first_hi):
-            group, name, pieces = items[i]
+            base, width, name, pieces = items[i]
             product = multiply(i, first_hi)
             for frame_tile, (frame, start, end) in zip(frame_tiles[name], pieces):
-                columns = slice(start - group * GROUP, end - group * GROUP)
+                columns = slice(start - base, end - base)
                 nc.vector.scalar_tensor_tensor(
                     out=frame_tile[:, first_hi : first_hi + BANK_HI, start - frame * FRAME : end - frame * FRAME],
                     in0=inv_norms[i][:, columns].unsqueeze(1).to_broadcast([P, BANK_HI, end - start]),
@@ -215,15 +237,15 @@ def tile_costvolumeattention17_pa_kernel(tc, x, q_w, k_w, out_0, out_1):
                 )
 
         def store(i):
-            group, name, pieces = items[i]
+            base, width, name, pieces = items[i]
             for frame_tile, (frame, start, end) in zip(list(frame_tiles[name]), pieces):
-                whole = not (name == "q" and frame == T - 1)
+                whole = (name, frame) not in PIECEWISE
                 for t in frames_fed(shifts[name], frame):
                     if whole and end == (frame + 1) * FRAME:
                         nc.sync.dma_start(out=outputs[name][t], in_=frame_tile[:].rearrange("p j n -> p (j n)"))
                     if not whole:
                         first, last = start - frame * FRAME, end - frame * FRAME
-                        nc.sync.dma_start(out=last_frame_q[:, :, first:last], in_=frame_tile[:, :, first:last])
+                        nc.sync.dma_start(out=by_channel[name][t][:, :, first:last], in_=frame_tile[:, :, first:last])
                 if end == (frame + 1) * FRAME:
                     frame_tiles[name] = frame_tiles[name][1:]
 

@@ -25,16 +25,13 @@ GROUP = 256
 GROUPS = (TOKENS + GROUP - 1) // GROUP
 BANK_HI = 2
 BLOCK = 4
-BLOCK_TOKENS = BLOCK * P
-BLOCKS = (TOKENS + BLOCK_TOKENS - 1) // BLOCK_TOKENS
+BLOCKS = 14
 BANK_ROWS = 2
 MAX_INV_NORM = 1.0e12
 LAG_SUM = 3
 LAG_NORM = 5
 LAG_SCALE = 5
-HEAD_STEPS = LAG_SCALE + 1
-HEAD_PARTS = 3
-LATER_PARTS = 1
+AHEAD = 4
 ALIGN = 64
 KEY_LEAD = 3
 PIECEWISE = [("k", T - 1), ("q", T - 2), ("q", T - 1)]
@@ -44,6 +41,17 @@ FLOPS = 2 * TOKENS * C * (2 * HEADS * D_LO * D_HI)
 
 def windows(start, end):
     return [(first, min(GROUP, end - first)) for first in range(start, end, GROUP)]
+
+
+def cut_sets(start, end):
+    cut = []
+    count = BLOCK
+    while start < end:
+        while start + count > end:
+            count //= 2
+        cut.append((start, count))
+        start += count
+    return cut
 
 
 def frame_pieces(start, width, frames):
@@ -88,6 +96,12 @@ def tile_costvolumeattention17_pa_kernel(tc, x, q_w, k_w, out_0, out_1):
         }
 
         last = T - 1
+        first_set = last * FRAME // P
+        blocks = [
+            (first, count)
+            for start, end in ((0, first_set), (first_set, TOKENS // P))
+            for first, count in cut_sets(start, end)
+        ]
         runs = [
             ("k", windows(last * FRAME // ALIGN * ALIGN, TOKENS), [last]),
             ("q", windows(0, TOKENS), range(T)),
@@ -111,23 +125,31 @@ def tile_costvolumeattention17_pa_kernel(tc, x, q_w, k_w, out_0, out_1):
         x_rows = x[0].rearrange("(a p) c -> p a c", p=P)
         weights = {"q": q_w, "k": k_w}
         jobs = []
+
+        def load_weights(name, first_hi, item):
+            w_rows = keep.tile([P, BANK_HI, C], BF16, name="w_rows_" + name + str(first_hi))
+            rows = weights[name].rearrange("(m j) c -> m j c", j=D_HI)
+            nc.sync.dma_start(out=w_rows[:], in_=rows[:, first_hi : first_hi + BANK_HI, :])
+            columns = slice(first_hi * P, (first_hi + BANK_HI) * P)
+            jobs.append((w_rows, w_codes[name][:, columns], w_scales[name][:, columns], item))
+
+        def load_tokens(first, count, item):
+            x_block = loads.tile([P, count, C], BF16, tag="x_block")
+            nc.sync.dma_start(out=x_block[:], in_=x_rows[:, first : first + count, :])
+            columns = slice(first * P, (first + count) * P)
+            jobs.append((x_block, x_codes[:, columns], x_scales[:, columns], item))
+
         seen = []
         for i, (start, width, name, pieces) in enumerate(items):
             if name not in seen:
+                load_weights(name, 0, i)
+            for first, count in blocks:
+                if first not in seen and first * P < start + width and start < (first + count) * P:
+                    seen.append(first)
+                    load_tokens(first, count, i)
+            if name not in seen:
                 seen.append(name)
-                w_rows = keep.tile([P, D_HI, C], BF16, name="w_rows_" + name)
-                nc.sync.dma_start(out=w_rows[:], in_=weights[name].rearrange("(m j) c -> m j c", j=D_HI))
-                jobs.append((w_rows, w_codes[name][:], w_scales[name][:], i))
-            for block in range(start // BLOCK_TOKENS, (start + width - 1) // BLOCK_TOKENS + 1):
-                if block in seen:
-                    continue
-                seen.append(block)
-                first = block * BLOCK
-                count = min(BLOCK, TOKENS // P - first)
-                x_block = loads.tile([P, count, C], BF16, tag="x_block")
-                nc.sync.dma_start(out=x_block[:], in_=x_rows[:, first : first + count, :])
-                columns = slice(first * P, (first + count) * P)
-                jobs.append((x_block, x_codes[:, columns], x_scales[:, columns], i))
+                load_weights(name, BANK_HI, i)
 
         identity = keep.tile([P, P], F32)
         make_identity(nc, identity[:])
@@ -138,6 +160,10 @@ def tile_costvolumeattention17_pa_kernel(tc, x, q_w, k_w, out_0, out_1):
             axis=mybir.AxisListType.X,
             op=ALU.add,
         )
+        one = keep.tile([P, 1], F32)
+        nc.gpsimd.memset(one[:], 1.0)
+        one_inverted = keep.tile([P, 1], F32)
+        nc.scalar.activation(out=one_inverted[:], in_=one[:], func=ACT.Abs_reciprocal_sqrt)
         ones_lo = keep.tile([P, HEADS, D_LO], F32)
         nc.vector.tensor_copy(out=ones_lo[:], in_=same_head[:].unsqueeze(2).to_broadcast([P, HEADS, D_LO]))
 
@@ -282,6 +308,7 @@ def tile_costvolumeattention17_pa_kernel(tc, x, q_w, k_w, out_0, out_1):
             prepare(parts[next_part], copies[next_part % 2])
             next_part += 1
 
+        waiting = []
         for step in range(len(items) + LAG_SCALE):
             new, old = step, step - LAG_SCALE
             if 0 <= step - LAG_NORM < len(items):
@@ -290,11 +317,15 @@ def tile_costvolumeattention17_pa_kernel(tc, x, q_w, k_w, out_0, out_1):
                 finish_sum(step - LAG_SUM)
             if 0 <= step - LAG_NORM < len(items):
                 invert_norm(step - LAG_NORM)
-            for j in range(HEAD_PARTS if step < HEAD_STEPS else LATER_PARTS):
-                if next_part < len(parts):
-                    by_vector = step < HEAD_STEPS or next_part % 4 == 0
-                    prepare(parts[next_part], nc.vector.tensor_copy if by_vector else nc.scalar.copy)
+            for part in waiting:
+                prepare(part, None)
+            waiting = []
+            if next_part < len(parts) and parts[next_part][0][3] <= step + AHEAD:
+                while parts[next_part][2] is not None:
+                    prepare(parts[next_part], copies[next_part % 2])
                     next_part += 1
+                waiting.append(parts[next_part])
+                next_part += 1
             if old >= 0:
                 open_frames(old)
             for first_hi in range(0, D_HI, BANK_HI):

@@ -30,11 +30,12 @@ BANK_ROWS = 2
 MAX_INV_NORM = 1.0e12
 LAG_SUM = 3
 LAG_NORM = 5
-LAG_SCALE = 5
+LAG_SCALE = 6
+HEAD_STEPS = 3
+MUST = 2
 AHEAD = 4
 ALIGN = 64
 KEY_LEAD = 3
-PIECEWISE = [("k", T - 1), ("q", T - 2), ("q", T - 1)]
 
 FLOPS = 2 * TOKENS * C * (2 * HEADS * D_LO * D_HI)
 
@@ -90,10 +91,6 @@ def tile_costvolumeattention17_pa_kernel(tc, x, q_w, k_w, out_0, out_1):
             "k": out_1.rearrange("(h t) (dlo dhi) i j -> t h dlo (dhi i j)", t=T, dlo=D_LO),
         }
         shifts = {"q": 0, "k": 1}
-        by_channel = {
-            "q": out_0.rearrange("(h t) d i j -> t h d (i j)", t=T),
-            "k": out_1.rearrange("(h t) d i j -> t h d (i j)", t=T),
-        }
 
         last = T - 1
         first_set = last * FRAME // P
@@ -265,14 +262,9 @@ def tile_costvolumeattention17_pa_kernel(tc, x, q_w, k_w, out_0, out_1):
         def store(i):
             base, width, name, pieces = items[i]
             for frame_tile, (frame, start, end) in zip(list(frame_tiles[name]), pieces):
-                whole = (name, frame) not in PIECEWISE
-                for t in frames_fed(shifts[name], frame):
-                    if whole and end == (frame + 1) * FRAME:
-                        nc.sync.dma_start(out=outputs[name][t], in_=frame_tile[:].rearrange("p j n -> p (j n)"))
-                    if not whole:
-                        first, last = start - frame * FRAME, end - frame * FRAME
-                        nc.sync.dma_start(out=by_channel[name][t][:, :, first:last], in_=frame_tile[:, :, first:last])
                 if end == (frame + 1) * FRAME:
+                    for t in frames_fed(shifts[name], frame):
+                        nc.sync.dma_start(out=outputs[name][t], in_=frame_tile[:].rearrange("p j n -> p (j n)"))
                     frame_tiles[name] = frame_tiles[name][1:]
 
         parts = []
@@ -309,6 +301,7 @@ def tile_costvolumeattention17_pa_kernel(tc, x, q_w, k_w, out_0, out_1):
             next_part += 1
 
         waiting = []
+        banks_copied = 0
         for step in range(len(items) + LAG_SCALE):
             new, old = step, step - LAG_SCALE
             if 0 <= step - LAG_NORM < len(items):
@@ -320,9 +313,11 @@ def tile_costvolumeattention17_pa_kernel(tc, x, q_w, k_w, out_0, out_1):
             for part in waiting:
                 prepare(part, None)
             waiting = []
-            if next_part < len(parts) and parts[next_part][0][3] <= step + AHEAD:
+            while next_part < len(parts) and parts[next_part][0][3] <= step + (MUST if waiting else AHEAD):
                 while parts[next_part][2] is not None:
-                    prepare(parts[next_part], copies[next_part % 2])
+                    by_vector = step < HEAD_STEPS or banks_copied % 2 == 0
+                    prepare(parts[next_part], nc.vector.tensor_copy if by_vector else nc.scalar.copy)
+                    banks_copied += 1
                     next_part += 1
                 waiting.append(parts[next_part])
                 next_part += 1

@@ -35,6 +35,8 @@ HEAD_STEPS = 3
 MUST = 2
 AHEAD = 4
 ALIGN = 64
+HELD_BANKS = 2
+HOLD_EVERY = 4
 KEY_LEAD = 3
 
 FLOPS = 2 * TOKENS * C * (2 * HEADS * D_LO * D_HI)
@@ -75,7 +77,8 @@ def tile_costvolumeattention17_pa_kernel(tc, x, q_w, k_w, out_0, out_1):
         stage = ctx.enter_context(tc.tile_pool(name="stage", bufs=3))
         norm = ctx.enter_context(tc.tile_pool(name="norm", bufs=4))
         frames = ctx.enter_context(tc.tile_pool(name="frames", bufs=3))
-        banks = ctx.enter_context(tc.psum_pool(name="banks", bufs=8))
+        banks = ctx.enter_context(tc.psum_pool(name="banks", bufs=8 - HELD_BANKS))
+        held_banks = ctx.enter_context(tc.psum_pool(name="held_banks", bufs=HELD_BANKS))
         ctx.enter_context(tc.manual_schedule())
 
         w_codes = {}
@@ -165,6 +168,7 @@ def tile_costvolumeattention17_pa_kernel(tc, x, q_w, k_w, out_0, out_1):
         nc.vector.tensor_copy(out=ones_lo[:], in_=same_head[:].unsqueeze(2).to_broadcast([P, HEADS, D_LO]))
 
         squares = {}
+        held = {}
         pair_sums = {}
         hi_sums = {}
         head_sums = {}
@@ -174,10 +178,13 @@ def tile_costvolumeattention17_pa_kernel(tc, x, q_w, k_w, out_0, out_1):
         def width_of(i):
             return items[i][1]
 
-        def multiply(i, first_hi):
+        def holds(i, first_hi):
+            return first_hi > 0 and i % HOLD_EVERY == 0
+
+        def multiply(i, first_hi, pool):
             base, width, name, pieces = items[i]
             tokens = slice(base, base + width)
-            product = banks.tile([P, BANK_HI, GROUP], F32, tag="bank")
+            product = pool.tile([P, BANK_HI, GROUP], F32, tag="bank")
             for j in range(BANK_HI):
                 channels = slice((first_hi + j) * P, (first_hi + j + 1) * P)
                 nc.tensor.matmul_mx(
@@ -195,7 +202,10 @@ def tile_costvolumeattention17_pa_kernel(tc, x, q_w, k_w, out_0, out_1):
             width = width_of(i)
             if first_hi == 0:
                 squares[i] = norm.tile([P, D_HI, GROUP], F32, name="squares", bufs=3)
-            product = multiply(i, first_hi)
+            if holds(i, first_hi):
+                product = held[i] = multiply(i, first_hi, held_banks)
+            else:
+                product = multiply(i, first_hi, banks)
             nc.scalar.activation(
                 out=squares[i][:, first_hi : first_hi + BANK_HI, 0:width],
                 in_=product[:, :, 0:width],
@@ -247,7 +257,7 @@ def tile_costvolumeattention17_pa_kernel(tc, x, q_w, k_w, out_0, out_1):
 
         def scale(i, first_hi):
             base, width, name, pieces = items[i]
-            product = multiply(i, first_hi)
+            product = held[i] if holds(i, first_hi) else multiply(i, first_hi, banks)
             for frame_tile, (frame, start, end) in zip(frame_tiles[name], pieces):
                 columns = slice(start - base, end - base)
                 nc.vector.scalar_tensor_tensor(
@@ -324,9 +334,9 @@ def tile_costvolumeattention17_pa_kernel(tc, x, q_w, k_w, out_0, out_1):
             if old >= 0:
                 open_frames(old)
             for first_hi in range(0, D_HI, BANK_HI):
+                if old >= 0:
+                    scale(old, D_HI - BANK_HI - first_hi)
                 if new < len(items):
                     square(new, first_hi)
-                if old >= 0:
-                    scale(old, first_hi)
             if old >= 0:
                 store(old)

@@ -26,18 +26,20 @@ GROUPS = (TOKENS + GROUP - 1) // GROUP
 BANK_HI = 2
 BLOCK = 4
 BLOCKS = 14
+HALF_STEPS = D_HI // BANK_HI
 BANK_ROWS = 2
 MAX_INV_NORM = 1.0e12
-LAG_SUM = 3
-LAG_NORM = 5
-LAG_SCALE = 6
+LAG_SUM = 6
+LAG_NORM = 10
+LAG_SCALE = 11
 HEAD_STEPS = 3
 MUST = 2
 AHEAD = 4
 ALIGN = 64
 HELD_BANKS = 2
-HOLD_EVERY = 4
-KEY_LEAD = 3
+HOLD_EVERY = 3
+FIRST_PART = 2
+KEY_LEAD = 2
 
 FLOPS = 2 * TOKENS * C * (2 * HEADS * D_LO * D_HI)
 
@@ -90,8 +92,8 @@ def tile_costvolumeattention17_pa_kernel(tc, x, q_w, k_w, out_0, out_1):
         x_scales = keep.tile([P, TOKENS], U8, align_bytes=64)
 
         outputs = {
-            "q": out_0.rearrange("(h t) (dlo dhi) i j -> t h dlo (dhi i j)", t=T, dlo=D_LO),
-            "k": out_1.rearrange("(h t) (dlo dhi) i j -> t h dlo (dhi i j)", t=T, dlo=D_LO),
+            "q": out_0.rearrange("(h t) d i j -> t h d (i j)", t=T),
+            "k": out_1.rearrange("(h t) d i j -> t h d (i j)", t=T),
         }
         shifts = {"q": 0, "k": 1}
 
@@ -174,6 +176,8 @@ def tile_costvolumeattention17_pa_kernel(tc, x, q_w, k_w, out_0, out_1):
         head_sums = {}
         inv_norms = {}
         frame_tiles = {}
+        items_done = {}
+        stored = {}
 
         def width_of(i):
             return items[i][1]
@@ -212,7 +216,7 @@ def tile_costvolumeattention17_pa_kernel(tc, x, q_w, k_w, out_0, out_1):
                 func=ACT.Square,
             )
             if first_hi + BANK_HI == D_HI:
-                pair_sums[i] = norm.tile([P, D_HI // 2, GROUP], F32, name="pair_sums", bufs=LAG_SUM + 2)
+                pair_sums[i] = norm.tile([P, D_HI // 2, GROUP], F32, name="pair_sums", bufs=LAG_SUM // 2 + 2)
                 nc.gpsimd.tensor_tensor(
                     out=pair_sums[i][:, :, 0:width],
                     in0=squares[i][:, 0:2, 0:width],
@@ -222,7 +226,7 @@ def tile_costvolumeattention17_pa_kernel(tc, x, q_w, k_w, out_0, out_1):
 
         def finish_sum(i):
             width = width_of(i)
-            hi_sums[i] = norm.tile([P, GROUP], F32, name="hi_sums", bufs=LAG_NORM - LAG_SUM + 2)
+            hi_sums[i] = norm.tile([P, GROUP], F32, name="hi_sums", bufs=(LAG_NORM - LAG_SUM) // 2 + 2)
             nc.vector.tensor_tensor(
                 out=hi_sums[i][:, 0:width],
                 in0=pair_sums[i][:, 0, 0:width],
@@ -243,7 +247,7 @@ def tile_costvolumeattention17_pa_kernel(tc, x, q_w, k_w, out_0, out_1):
 
         def invert_norm(i):
             width = width_of(i)
-            inv_norms[i] = norm.tile([P, GROUP], F32, name="inv_norm", bufs=LAG_SCALE - LAG_NORM + 2)
+            inv_norms[i] = norm.tile([P, GROUP], F32, name="inv_norm", bufs=3)
             nc.scalar.activation(
                 out=inv_norms[i][:, 0:width], in_=head_sums[i][:, 0:width], func=ACT.Abs_reciprocal_sqrt
             )
@@ -272,9 +276,14 @@ def tile_costvolumeattention17_pa_kernel(tc, x, q_w, k_w, out_0, out_1):
         def store(i):
             base, width, name, pieces = items[i]
             for frame_tile, (frame, start, end) in zip(list(frame_tiles[name]), pieces):
-                if end == (frame + 1) * FRAME:
+                complete = end == (frame + 1) * FRAME
+                items_done[name, frame] = items_done.get((name, frame), 0) + 1
+                if items_done[name, frame] == FIRST_PART or complete:
+                    first, last = stored.get((name, frame), 0), end - frame * FRAME
+                    stored[name, frame] = last
                     for t in frames_fed(shifts[name], frame):
-                        nc.sync.dma_start(out=outputs[name][t], in_=frame_tile[:].rearrange("p j n -> p (j n)"))
+                        nc.sync.dma_start(out=outputs[name][t][:, :, first:last], in_=frame_tile[:, :, first:last])
+                if complete:
                     frame_tiles[name] = frame_tiles[name][1:]
 
         parts = []
@@ -310,20 +319,25 @@ def tile_costvolumeattention17_pa_kernel(tc, x, q_w, k_w, out_0, out_1):
             prepare(parts[next_part], copies[next_part % 2])
             next_part += 1
 
+        def due(half_step, lag):
+            i, rest = divmod(half_step - lag, HALF_STEPS)
+            return [i] if rest == 0 and 0 <= i < len(items) else []
+
         waiting = []
         banks_copied = 0
-        for step in range(len(items) + LAG_SCALE):
-            new, old = step, step - LAG_SCALE
-            if 0 <= step - LAG_NORM < len(items):
-                sum_heads(step - LAG_NORM)
-            if 0 <= step - LAG_SUM < len(items):
-                finish_sum(step - LAG_SUM)
-            if 0 <= step - LAG_NORM < len(items):
-                invert_norm(step - LAG_NORM)
-            for part in waiting:
-                prepare(part, None)
-            waiting = []
-            while next_part < len(parts) and parts[next_part][0][3] <= step + (MUST if waiting else AHEAD):
+        for half_step in range(HALF_STEPS * len(items) + LAG_SCALE):
+            step, half = divmod(half_step, HALF_STEPS)
+            for i in due(half_step, LAG_NORM):
+                sum_heads(i)
+            for i in due(half_step, LAG_SUM):
+                finish_sum(i)
+            for i in due(half_step, LAG_NORM):
+                invert_norm(i)
+            if half == 0:
+                for part in waiting:
+                    prepare(part, None)
+                waiting = []
+            while half == 0 and next_part < len(parts) and parts[next_part][0][3] <= step + (MUST if waiting else AHEAD):
                 while parts[next_part][2] is not None:
                     by_vector = step < HEAD_STEPS or banks_copied % 2 == 0
                     prepare(parts[next_part], nc.vector.tensor_copy if by_vector else nc.scalar.copy)
@@ -331,12 +345,12 @@ def tile_costvolumeattention17_pa_kernel(tc, x, q_w, k_w, out_0, out_1):
                     next_part += 1
                 waiting.append(parts[next_part])
                 next_part += 1
-            if old >= 0:
-                open_frames(old)
-            for first_hi in range(0, D_HI, BANK_HI):
-                if old >= 0:
-                    scale(old, D_HI - BANK_HI - first_hi)
-                if new < len(items):
-                    square(new, first_hi)
-            if old >= 0:
-                store(old)
+            for i in due(half_step, LAG_SCALE):
+                open_frames(i)
+                scale(i, BANK_HI)
+            for i in due(half_step, LAG_SCALE + 1):
+                scale(i, 0)
+            if step < len(items):
+                square(step, half * BANK_HI)
+            for i in due(half_step, LAG_SCALE + 1):
+                store(i)

from contextlib import ExitStack

import concourse.mybir as mybir
from concourse.masks import make_identity

F32 = mybir.dt.float32
BF16 = mybir.dt.bfloat16
U32 = mybir.dt.uint32
U8 = mybir.dt.uint8
FP8X4 = mybir.dt.float8_e4m3fn_x4
ALU = mybir.AluOpType
ACT = mybir.ActivationFunctionType

P = 128
PACK = 4
HALVES = 2
C = 512
T = 8
FRAME = 784
TOKENS = T * FRAME
HEADS = 32
D_LO = 4
D_HI = 4
GROUP = 256
GROUPS = (TOKENS + GROUP - 1) // GROUP
BANK_HI = 2
BLOCK = 4
BLOCKS = 14
HALF_STEPS = D_HI // BANK_HI
BANK_ROWS = 2
MAX_INV_NORM = 1.0e12
LAG_SUM = 6
LAG_NORM = 10
LAG_SCALE = 11
HEAD_STEPS = 3
MUST = 2
AHEAD = 4
ALIGN = 64
HELD_BANKS = 2
HOLD_EVERY = 3
FIRST_PART = 2
KEY_LEAD = 2

FLOPS = 2 * TOKENS * C * (2 * HEADS * D_LO * D_HI)


def windows(start, end):
    return [(first, min(GROUP, end - first)) for first in range(start, end, GROUP)]


def cut_sets(start, end):
    cut = []
    count = BLOCK
    while start < end:
        while start + count > end:
            count //= 2
        cut.append((start, count))
        start += count
    return cut


def frame_pieces(start, width, frames):
    return [
        (frame, max(start, frame * FRAME), min(start + width, (frame + 1) * FRAME))
        for frame in frames
        if start < (frame + 1) * FRAME and frame * FRAME < start + width
    ]


def frames_fed(shift, frame):
    return [t for t in range(T) if min(t + shift, T - 1) == frame]


def tile_costvolumeattention17_pa_kernel(tc, x, q_w, k_w, out_0, out_1):
    nc = tc.nc
    with ExitStack() as ctx:
        keep = ctx.enter_context(tc.tile_pool(name="keep", bufs=1))
        loads = ctx.enter_context(tc.tile_pool(name="loads", bufs=BLOCKS))
        stage = ctx.enter_context(tc.tile_pool(name="stage", bufs=3))
        norm = ctx.enter_context(tc.tile_pool(name="norm", bufs=4))
        frames = ctx.enter_context(tc.tile_pool(name="frames", bufs=3))
        banks = ctx.enter_context(tc.psum_pool(name="banks", bufs=8 - HELD_BANKS))
        held_banks = ctx.enter_context(tc.psum_pool(name="held_banks", bufs=HELD_BANKS))
        ctx.enter_context(tc.manual_schedule())

        w_codes = {}
        w_scales = {}
        for name in ("q", "k"):
            w_codes[name] = keep.tile([P, D_HI * P], U32, align_bytes=64, name="w_codes_" + name)
            w_scales[name] = keep.tile([P, D_HI * P], U8, align_bytes=64, name="w_scales_" + name)
        x_codes = keep.tile([P, TOKENS], U32, align_bytes=64)
        x_scales = keep.tile([P, TOKENS], U8, align_bytes=64)

        outputs = {
            "q": out_0.rearrange("(h t) d i j -> t h d (i j)", t=T),
            "k": out_1.rearrange("(h t) d i j -> t h d (i j)", t=T),
        }
        shifts = {"q": 0, "k": 1}

        last = T - 1
        first_set = last * FRAME // P
        blocks = [
            (first, count)
            for start, end in ((0, first_set), (first_set, TOKENS // P))
            for first, count in cut_sets(start, end)
        ]
        runs = [
            ("k", windows(last * FRAME // ALIGN * ALIGN, TOKENS), [last]),
            ("q", windows(0, TOKENS), range(T)),
            ("k", windows(FRAME // ALIGN * ALIGN, -(-last * FRAME // ALIGN) * ALIGN), range(1, last)),
        ]
        order = [("k", last)]
        for frame in range(T):
            order.append(("q", frame))
            if frame + KEY_LEAD < last:
                order.append(("k", frame + KEY_LEAD))
            if frame == 0:
                order[1:1] = [("k", f) for f in range(1, KEY_LEAD)]
        items = []
        for name, frame in order:
            for run_name, run, run_frames in runs:
                for start, width in run:
                    pieces = frame_pieces(start, width, run_frames)
                    if run_name == name and pieces[-1][0] == frame:
                        items.append((start, width, name, pieces))

        x_rows = x[0].rearrange("(a p) c -> p a c", p=P)
        weights = {"q": q_w, "k": k_w}
        jobs = []

        def load_weights(name, first_hi, item):
            w_rows = keep.tile([P, BANK_HI, C], BF16, name="w_rows_" + name + str(first_hi))
            rows = weights[name].rearrange("(m j) c -> m j c", j=D_HI)
            nc.sync.dma_start(out=w_rows[:], in_=rows[:, first_hi : first_hi + BANK_HI, :])
            columns = slice(first_hi * P, (first_hi + BANK_HI) * P)
            jobs.append((w_rows, w_codes[name][:, columns], w_scales[name][:, columns], item))

        def load_tokens(first, count, item):
            x_block = loads.tile([P, count, C], BF16, tag="x_block")
            nc.sync.dma_start(out=x_block[:], in_=x_rows[:, first : first + count, :])
            columns = slice(first * P, (first + count) * P)
            jobs.append((x_block, x_codes[:, columns], x_scales[:, columns], item))

        seen = []
        for i, (start, width, name, pieces) in enumerate(items):
            if name not in seen:
                load_weights(name, 0, i)
            for first, count in blocks:
                if first not in seen and first * P < start + width and start < (first + count) * P:
                    seen.append(first)
                    load_tokens(first, count, i)
            if name not in seen:
                seen.append(name)
                load_weights(name, BANK_HI, i)

        identity = keep.tile([P, P], F32)
        make_identity(nc, identity[:])
        same_head = keep.tile([P, HEADS], F32)
        nc.vector.tensor_reduce(
            out=same_head[:],
            in_=identity[:].rearrange("p (h i) -> p h i", i=D_LO),
            axis=mybir.AxisListType.X,
            op=ALU.add,
        )
        one = keep.tile([P, 1], F32)
        nc.gpsimd.memset(one[:], 1.0)
        one_inverted = keep.tile([P, 1], F32)
        nc.scalar.activation(out=one_inverted[:], in_=one[:], func=ACT.Abs_reciprocal_sqrt)
        ones_lo = keep.tile([P, HEADS, D_LO], F32)
        nc.vector.tensor_copy(out=ones_lo[:], in_=same_head[:].unsqueeze(2).to_broadcast([P, HEADS, D_LO]))

        squares = {}
        held = {}
        pair_sums = {}
        hi_sums = {}
        head_sums = {}
        inv_norms = {}
        frame_tiles = {}
        items_done = {}
        stored = {}

        def width_of(i):
            return items[i][1]

        def holds(i, first_hi):
            return first_hi > 0 and i % HOLD_EVERY == 0

        def multiply(i, first_hi, pool):
            base, width, name, pieces = items[i]
            tokens = slice(base, base + width)
            product = pool.tile([P, BANK_HI, GROUP], F32, tag="bank")
            for j in range(BANK_HI):
                channels = slice((first_hi + j) * P, (first_hi + j + 1) * P)
                nc.tensor.matmul_mx(
                    out=product[:, j, 0 : width_of(i)],
                    lhsT=w_codes[name][:, channels].bitcast(FP8X4),
                    lhsT_scale=w_scales[name][:, channels],
                    rhs=x_codes[:, tokens].bitcast(FP8X4),
                    rhs_scale=x_scales[:, tokens],
                    start=True,
                    stop=True,
                )
            return product

        def square(i, first_hi):
            width = width_of(i)
            if first_hi == 0:
                squares[i] = norm.tile([P, D_HI, GROUP], F32, name="squares", bufs=3)
            if holds(i, first_hi):
                product = held[i] = multiply(i, first_hi, held_banks)
            else:
                product = multiply(i, first_hi, banks)
            nc.scalar.activation(
                out=squares[i][:, first_hi : first_hi + BANK_HI, 0:width],
                in_=product[:, :, 0:width],
                func=ACT.Square,
            )
            if first_hi + BANK_HI == D_HI:
                pair_sums[i] = norm.tile([P, D_HI // 2, GROUP], F32, name="pair_sums", bufs=LAG_SUM // 2 + 2)
                nc.gpsimd.tensor_tensor(
                    out=pair_sums[i][:, :, 0:width],
                    in0=squares[i][:, 0:2, 0:width],
                    in1=squares[i][:, 2:4, 0:width],
                    op=ALU.add,
                )

        def finish_sum(i):
            width = width_of(i)
            hi_sums[i] = norm.tile([P, GROUP], F32, name="hi_sums", bufs=(LAG_NORM - LAG_SUM) // 2 + 2)
            nc.vector.tensor_tensor(
                out=hi_sums[i][:, 0:width],
                in0=pair_sums[i][:, 0, 0:width],
                in1=pair_sums[i][:, 1, 0:width],
                op=ALU.add,
            )

        def sum_heads(i):
            width = width_of(i)
            head_sums[i] = banks.tile([P, GROUP], F32, name="head_sums", tag="bank")
            nc.tensor.matmul(
                out=head_sums[i][:, 0:width],
                lhsT=ones_lo[:].rearrange("p h i -> p (h i)"),
                rhs=hi_sums[i][:, 0:width],
                start=True,
                stop=True,
            )

        def invert_norm(i):
            width = width_of(i)
            inv_norms[i] = norm.tile([P, GROUP], F32, name="inv_norm", bufs=3)
            nc.scalar.activation(
                out=inv_norms[i][:, 0:width], in_=head_sums[i][:, 0:width], func=ACT.Abs_reciprocal_sqrt
            )

        def open_frames(i):
            base, width, name, pieces = items[i]
            if pieces[0][1] == pieces[0][0] * FRAME:
                frame_tiles[name] = [frames.tile([P, D_HI, FRAME], F32, name="frame_" + name)]
            if len(pieces) > 1:
                frame_tiles[name].append(frames.tile([P, D_HI, FRAME], F32, name="frame_" + name))

        def scale(i, first_hi):
            base, width, name, pieces = items[i]
            product = held[i] if holds(i, first_hi) else multiply(i, first_hi, banks)
            for frame_tile, (frame, start, end) in zip(frame_tiles[name], pieces):
                columns = slice(start - base, end - base)
                nc.vector.scalar_tensor_tensor(
                    out=frame_tile[:, first_hi : first_hi + BANK_HI, start - frame * FRAME : end - frame * FRAME],
                    in0=inv_norms[i][:, columns].unsqueeze(1).to_broadcast([P, BANK_HI, end - start]),
                    scalar=MAX_INV_NORM,
                    in1=product[:, :, columns],
                    op0=ALU.min,
                    op1=ALU.mult,
                )

        def store(i):
            base, width, name, pieces = items[i]
            for frame_tile, (frame, start, end) in zip(list(frame_tiles[name]), pieces):
                complete = end == (frame + 1) * FRAME
                items_done[name, frame] = items_done.get((name, frame), 0) + 1
                if items_done[name, frame] == FIRST_PART or complete:
                    first, last = stored.get((name, frame), 0), end - frame * FRAME
                    stored[name, frame] = last
                    for t in frames_fed(shifts[name], frame):
                        nc.sync.dma_start(out=outputs[name][t][:, :, first:last], in_=frame_tile[:, :, first:last])
                if complete:
                    frame_tiles[name] = frame_tiles[name][1:]

        parts = []
        for job in jobs:
            grouped = []
            for first in range(0, job[0].shape[1], BANK_ROWS):
                parts.append((job, grouped, first))
            parts.append((job, grouped, None))

        def prepare(part, copy_out):
            (rows, codes, scales, first_item), grouped, first = part
            sets = rows.shape[1]
            if not grouped:
                grouped.append(stage.tile([P, BLOCK * P * PACK], BF16, align_bytes=64, name="grouped"))
            if first is None:
                nc.vector.quantize_mx(out=codes.bitcast(FP8X4), scales=scales, in_=grouped[0][:, 0 : sets * P * PACK])
                return
            grouped_words = grouped[0][:].bitcast(F32).rearrange("p (g r u) -> p g r u", r=P, u=HALVES)
            count = min(BANK_ROWS, sets - first)
            turned = banks.tile([P, BANK_ROWS, HALVES, P], F32, tag="bank")
            for g in range(count):
                row_words = rows[:, first + g, :].bitcast(F32)
                for u in range(HALVES):
                    nc.tensor.transpose(turned[:, g, u, :], row_words[:, u::HALVES], identity[:])
            copy_out(
                grouped_words[:, first : first + count],
                turned[:, 0:count].rearrange("p g u r -> p g r u"),
            )

        copies = (nc.vector.tensor_copy, nc.scalar.copy)
        next_part = 0
        while parts[next_part][0][3] == 0:
            prepare(parts[next_part], copies[next_part % 2])
            next_part += 1

        def due(half_step, lag):
            i, rest = divmod(half_step - lag, HALF_STEPS)
            return [i] if rest == 0 and 0 <= i < len(items) else []

        waiting = []
        banks_copied = 0
        for half_step in range(HALF_STEPS * len(items) + LAG_SCALE):
            step, half = divmod(half_step, HALF_STEPS)
            for i in due(half_step, LAG_NORM):
                sum_heads(i)
            for i in due(half_step, LAG_SUM):
                finish_sum(i)
            for i in due(half_step, LAG_NORM):
                invert_norm(i)
            if half == 0:
                for part in waiting:
                    prepare(part, None)
                waiting = []
            while half == 0 and next_part < len(parts) and parts[next_part][0][3] <= step + (MUST if waiting else AHEAD):
                while parts[next_part][2] is not None:
                    by_vector = step < HEAD_STEPS or banks_copied % 2 == 0
                    prepare(parts[next_part], nc.vector.tensor_copy if by_vector else nc.scalar.copy)
                    banks_copied += 1
                    next_part += 1
                waiting.append(parts[next_part])
                next_part += 1
            for i in due(half_step, LAG_SCALE):
                open_frames(i)
                scale(i, BANK_HI)
            for i in due(half_step, LAG_SCALE + 1):
                scale(i, 0)
            if step < len(items):
                square(step, half * BANK_HI)
            for i in due(half_step, LAG_SCALE + 1):
                store(i)
